import numpy as np
import ml_dtypes


def mxq(x, axis, fmt="e4m3"):
    dtype, down = {"e4m3": (ml_dtypes.float8_e4m3fn, 7), "e5m2": (ml_dtypes.float8_e5m2, 14)}[fmt]
    v = np.moveaxis(np.asarray(x, np.float32).astype(ml_dtypes.bfloat16).astype(np.float64), axis, -1)
    blocks = v.reshape(v.shape[:-1] + (-1, 32))
    amax = np.abs(blocks).max(-1, keepdims=True)
    byte = np.maximum(np.where(amax > 0, np.frexp(amax)[1] - 1 + 127, 0) - down, 1)
    scale = np.exp2(byte - 127.0)
    codes = (blocks / scale).astype(np.float32).astype(dtype).astype(np.float64)
    return np.moveaxis((codes * scale).reshape(v.shape), -1, axis)


WIDE = False


def mx_kscale(k):
    if not WIDE:
        return np.ones(k)
    levels = np.array([10, -10, 5, -5, 0])
    if k % 512:
        return np.exp2(np.random.permutation(np.resize(levels, k // 32))).repeat(32)
    a = np.empty((k // 512, 16))
    for p in range(k // 512):
        a[p, :8] = np.random.permutation(np.resize(levels, 8))
        for g in range(8):
            far = levels[np.abs(levels - a[p, g]) >= 10]
            a[p, g + 8] = far[np.random.randint(len(far))]
    return np.exp2(a.ravel()).repeat(32)


BF16 = ml_dtypes.bfloat16


def bf(x):
    return np.asarray(x, np.float32).astype(BF16)


def f64(x):
    return np.asarray(x).astype(np.float64)


B, S, H, I, G = 4, 1024, 512, 1024, 4
T = B * S


def grouped_linear(xf, w, b):
    g, dout, din = w.shape
    xg = xf.reshape(g, -1, din)
    y = (mxq(xg, 2, "e4m3") @ mxq(w, 2, "e4m3").transpose(0, 2, 1)) + b[:, None, :]
    return y.reshape(-1, dout)


def setup_inputs():
    s, t = mx_kscale(H), mx_kscale(I)
    return {"hf": bf(np.random.standard_normal((T, H)) * s),
            "g1_w": bf(np.random.standard_normal((G, I, H)) / np.sqrt(H) / s[None, None, :] * t[None, :, None]),
            "g1_b": bf(np.random.standard_normal((G, I)) * 0.3 * t[None, :]),
            "g2_w": bf(np.random.standard_normal((G, H, I)) / np.sqrt(I) / t[None, None, :]),
            "g2_b": bf(np.random.standard_normal((G, H)) * 0.3)}


def reference(hf, g1_w, g1_b, g2_w, g2_b):
    y = grouped_linear(f64(hf), f64(g1_w), f64(g1_b))
    return grouped_linear(y, f64(g2_w), f64(g2_b))

@@ -1,0 +1,261 @@
+from contextlib import ExitStack
+
+import concourse.mybir as mybir
+from concourse.masks import make_identity
+
+F32 = mybir.dt.float32
+BF16 = mybir.dt.bfloat16
+U32 = mybir.dt.uint32
+U8 = mybir.dt.uint8
+FP8X4 = mybir.dt.float8_e4m3fn_x4
+
+P = 128
+PACK = 4
+K_PASS = P * PACK
+WORDS = K_PASS // 2
+BANK = 512
+
+GROUPS, TOKENS, HIDDEN, INNER = 4, 4096, 512, 1024
+GROUP_TOKENS = TOKENS // GROUPS
+CHUNK = 512
+CHUNKS = TOKENS // CHUNK
+CHUNKS_PER_GROUP = GROUP_TOKENS // CHUNK
+BLOCKS = CHUNK // P
+PASSES_2 = INNER // K_PASS
+INNER_TILES = INNER // P
+
+LEAD = 4
+UNITS_PER_ROUND = 3
+ROUNDS_WITH_HELP = 1
+BIAS2_BEHIND = (1, 0)
+
+FLOPS = 2 * TOKENS * HIDDEN * INNER * 2
+
+
+def tile_dummytemodel_pa_t_kernel(tc, hf, g1_w, g1_b, g2_w, g2_b, out):
+    nc = tc.nc
+    with ExitStack() as ctx:
+        const = ctx.enter_context(tc.tile_pool(name="const", bufs=1))
+        inputs = ctx.enter_context(tc.tile_pool(name="inputs", bufs=1))
+        grouped_pool = ctx.enter_context(tc.tile_pool(name="grouped", bufs=3))
+        codes_pool = ctx.enter_context(tc.tile_pool(name="codes", bufs=4))
+        y_pool = ctx.enter_context(tc.tile_pool(name="y", bufs=3))
+        out_pool = ctx.enter_context(tc.tile_pool(name="outs", bufs=12))
+        psum_scalar = ctx.enter_context(tc.psum_pool(name="psum_scalar", bufs=5))
+        psum_vector = ctx.enter_context(tc.psum_pool(name="psum_vector", bufs=3))
+        ctx.enter_context(tc.manual_schedule())
+
+        hf_view = hf.rearrange("(g r a) k -> g r a k", g=GROUPS, r=P)
+        out_view = out.rearrange("(g r a) h -> g r a h", g=GROUPS, r=P)
+        w1_view = g1_w.rearrange("g (c r t) k -> g r c (t k)", r=P, t=PACK)
+        w2_view = g2_w.rearrange("g (b r) i -> g r b i", r=P)
+
+        x_sb = [inputs.tile([P, BLOCKS, HIDDEN], BF16, name="x_sb%d" % s) for s in range(CHUNKS)]
+        w1_sb = [inputs.tile([P, INNER_TILES, HIDDEN], BF16, name="w1_sb%d" % g) for g in range(GROUPS)]
+        w2_sb = [inputs.tile([P, HIDDEN // P, INNER], BF16, name="w2_sb%d" % g) for g in range(GROUPS)]
+
+        b1_rows = const.tile([P, WORDS], F32)
+        nc.vector.memset(b1_rows[:], 0.0)
+        nc.scalar.dma_start(
+            out=b1_rows[:].bitcast(BF16)[0 : GROUPS * PASSES_2, :],
+            in_=g1_b.rearrange("g (c w) -> (g c) w", w=K_PASS),
+        )
+        b2_all = const.tile([P, GROUPS * HIDDEN], BF16)
+
+        def load_x(s):
+            g, n = divmod(s, CHUNKS_PER_GROUP)
+            for half in range(2):
+                nc.sync.dma_start(
+                    out=x_sb[s][:, 2 * half : 2 * half + 2, :],
+                    in_=hf_view[g, :, n * BLOCKS + 2 * half : n * BLOCKS + 2 * half + 2, :],
+                )
+
+        def load_w1(g, c):
+            for u in range(2):
+                nc.sync.dma_start(
+                    out=w1_sb[g][:, PACK * c + 2 * u : PACK * c + 2 * u + 2, :].rearrange("p e k -> p (e k)"),
+                    in_=w1_view[g, :, c, 2 * u * HIDDEN : 2 * (u + 1) * HIDDEN],
+                )
+
+        for g in range(GROUPS):
+            load_x(CHUNKS_PER_GROUP * g)
+            for c in range(PASSES_2):
+                load_w1(g, c)
+                if (g, c) == BIAS2_BEHIND:
+                    nc.sync.dma_start(out=b2_all[:], in_=g2_b.rearrange("g h -> (g h)").partition_broadcast(P))
+            load_x(CHUNKS_PER_GROUP * g + 1)
+            nc.sync.dma_start(out=w2_sb[g][:], in_=w2_view[g])
+
+        ident = const.tile([P, P], F32)
+        make_identity(nc, ident[:])
+
+        b1_words = const.tile([P, GROUPS * PASSES_2, 2], F32)
+        b1_col = const.tile([P, GROUPS * INNER_TILES], F32)
+
+        def transpose_bias():
+            b1_bank = psum_scalar.tile([P, BANK], F32, tag="bank")
+            planes = b1_bank[:].rearrange("p (u r) -> p u r", r=P)
+            for u in range(2):
+                nc.tensor.transpose(planes[:, u, :], b1_rows[:, u:WORDS:2], ident[:])
+            nc.vector.tensor_copy(
+                out=b1_words[:], in_=planes[:, 0:2, 0 : GROUPS * PASSES_2].rearrange("p u r -> p r u")
+            )
+            nc.vector.tensor_copy(out=b1_col[:], in_=b1_words[:].rearrange("p r u -> p (r u)").bitcast(BF16))
+
+        def unit_blocks(key):
+            kind = key[0]
+            if kind == "x":
+                words = x_sb[key[1]][:].bitcast(F32)
+                return [words[:, a, :] for a in range(BLOCKS)]
+            if kind == "w1":
+                words = w1_sb[key[1]][:].bitcast(F32)
+                return [words[:, PACK * key[2] + j, :] for j in range(PACK)]
+            words = w2_sb[key[1]][:].bitcast(F32)
+            return [words[:, b, WORDS * key[2] : WORDS * (key[2] + 1)] for b in range(HIDDEN // P)]
+
+        grouped = {}
+        codes = {}
+
+        def transpose_unit(key):
+            blocks = unit_blocks(key)
+            unit_bf16 = grouped_pool.tile([P, CHUNK, PACK], BF16, tag="unit_bf16", align_bytes=64)
+            unit_words = unit_bf16[:].bitcast(F32)
+            for half in range(2):
+                bank = psum_scalar.tile([P, BANK], F32, tag="bank")
+                planes = bank[:].rearrange("p (b u r) -> p b u r", b=2, u=2)
+                for b in range(2):
+                    for u in range(2):
+                        nc.tensor.transpose(planes[:, b, u, :], blocks[2 * half + b][:, u:WORDS:2], ident[:])
+                nc.scalar.copy(
+                    out=unit_words[:, 2 * P * half : 2 * P * (half + 1), :].rearrange("p (b r) u -> p b r u", b=2),
+                    in_=planes.rearrange("p b u r -> p b r u"),
+                )
+            grouped[key] = unit_bf16
+
+        def quantise(key):
+            tag = key[0]
+            words = codes_pool.tile([P, CHUNK], U32, tag=tag + "_words", align_bytes=64)
+            scales = codes_pool.tile([P, CHUNK], U8, tag=tag + "_scales", align_bytes=64)
+            nc.vector.quantize_mx(
+                out=words[:].bitcast(FP8X4),
+                scales=scales[:],
+                in_=grouped[key][:].rearrange("p c j -> p (c j)"),
+            )
+            codes[key] = (words, scales)
+
+        planar = {}
+
+        def layer1(s, c):
+            g = s // CHUNKS_PER_GROUP
+            x_words, x_scales = codes[("x", s)]
+            w_words, w_scales = codes[("w1", g, c)]
+            y_planar = y_pool.tile([P, PACK, CHUNK], BF16, tag="y_planar")
+            for j in range(PACK):
+                acc1 = psum_scalar.tile([P, BANK], F32, tag="bank")
+                nc.tensor.matmul_mx(
+                    out=acc1[:],
+                    lhsT=w_words[:, j * P : (j + 1) * P].bitcast(FP8X4),
+                    lhsT_scale=w_scales[:, j * P : (j + 1) * P],
+                    rhs=x_words[:].bitcast(FP8X4),
+                    rhs_scale=x_scales[:],
+                    start=True,
+                    stop=True,
+                )
+                column = INNER_TILES * g + PACK * c + j
+                if s < ROUNDS_WITH_HELP and j % 2 == 1:
+                    nc.vector.tensor_scalar(
+                        out=y_planar[:, j, :],
+                        in0=acc1[:],
+                        scalar1=b1_col[:, column : column + 1],
+                        scalar2=None,
+                        op0=mybir.AluOpType.add,
+                    )
+                else:
+                    nc.scalar.activation(
+                        out=y_planar[:, j, :],
+                        in_=acc1[:],
+                        func=mybir.ActivationFunctionType.Identity,
+                        bias=b1_col[:, column : column + 1],
+                    )
+            planar[(s, c)] = y_planar
+
+        def regroup_y(s, c):
+            y_bf16 = y_pool.tile([P, CHUNK, PACK], BF16, tag="y_bf16", align_bytes=64)
+            nc.vector.tensor_copy(
+                out=y_bf16[:].rearrange("p (t i) j -> p t j i", i=4),
+                in_=planar[(s, c)][:].rearrange("p j (t i) -> p t j i", i=4),
+            )
+            grouped[("y", s, c)] = y_bf16
+
+        def layer2(s, b):
+            g, n = divmod(s, CHUNKS_PER_GROUP)
+            acc2 = psum_vector.tile([P, HIDDEN], F32, tag="acc2")
+            for c in range(PASSES_2):
+                y_words, y_scales = codes[("y", s, c)]
+                w_words, w_scales = codes[("w2", g, c)]
+                nc.tensor.matmul_mx(
+                    out=acc2[:],
+                    lhsT=y_words[:, b * P : (b + 1) * P].bitcast(FP8X4),
+                    lhsT_scale=y_scales[:, b * P : (b + 1) * P],
+                    rhs=w_words[:].bitcast(FP8X4),
+                    rhs_scale=w_scales[:],
+                    start=(c == 0),
+                    stop=(c == PASSES_2 - 1),
+                )
+            result = out_pool.tile([P, HIDDEN], F32, tag="result")
+            nc.vector.tensor_tensor(
+                out=result[:],
+                in0=acc2[:],
+                in1=b2_all[:, g * HIDDEN : (g + 1) * HIDDEN],
+                op=mybir.AluOpType.add,
+            )
+            nc.sync.dma_start(out=out_view[g, :, n * BLOCKS + b, :], in_=result[:])
+
+        units = []
+        for g in range(GROUPS):
+            units.append(("x", CHUNKS_PER_GROUP * g))
+            units.extend([("w1", g, c) for c in range(PASSES_2)])
+            units.append(("x", CHUNKS_PER_GROUP * g + 1))
+            units.extend([("w2", g, c) for c in range(PASSES_2)])
+
+        for i in range(LEAD):
+            transpose_unit(units[i])
+            if i == 0:
+                transpose_bias()
+            else:
+                quantise(units[i - 1])
+        quantise(units[LEAD - 1])
+
+        for s in range(CHUNKS + 1):
+            first = LEAD + UNITS_PER_ROUND * s
+            unit_a, unit_b, unit_c = units[first : first + 1], units[first + 1 : first + 2], units[first + 2 : first + 3]
+            here, behind = s < CHUNKS, s > 0
+            if here:
+                layer1(s, 0)
+            for key in unit_a:
+                transpose_unit(key)
+            if behind:
+                layer2(s - 1, 0)
+            if here:
+                regroup_y(s, 0)
+            for key in unit_a:
+                quantise(key)
+            if here:
+                layer1(s, 1)
+            if behind:
+                layer2(s - 1, 1)
+            if here:
+                quantise(("y", s, 0))
+            for key in unit_b + unit_c:
+                transpose_unit(key)
+            if here:
+                regroup_y(s, 1)
+            for key in unit_b:
+                quantise(key)
+            if here:
+                quantise(("y", s, 1))
+            for key in unit_c:
+                quantise(key)
+            if behind:
+                layer2(s - 1, 2)
+                layer2(s - 1, 3)

@@ -26,8 +26,11 @@ INNER_TILES = INNER // P
 
 LEAD = 4
 UNITS_PER_ROUND = 3
-ROUNDS_WITH_HELP = 1
-BIAS2_BEHIND = (1, 0)
+LAG = 2
+QUARTERS = 4
+BIAS2_BEHIND = ("w1", 1, 0)
+
+SCALAR, VECTOR = "scalar", "vector"
 
 FLOPS = 2 * TOKENS * HIDDEN * INNER * 2
 
@@ -37,8 +40,8 @@ def tile_dummytemodel_pa_t_kernel(tc, hf, g1_w, g1_b, g2_w, g2_b, out):
     with ExitStack() as ctx:
         const = ctx.enter_context(tc.tile_pool(name="const", bufs=1))
         inputs = ctx.enter_context(tc.tile_pool(name="inputs", bufs=1))
-        grouped_pool = ctx.enter_context(tc.tile_pool(name="grouped", bufs=3))
-        codes_pool = ctx.enter_context(tc.tile_pool(name="codes", bufs=4))
+        grouped_pool = ctx.enter_context(tc.tile_pool(name="grouped", bufs=4))
+        codes_pool = ctx.enter_context(tc.tile_pool(name="codes", bufs=6))
         y_pool = ctx.enter_context(tc.tile_pool(name="y", bufs=3))
         out_pool = ctx.enter_context(tc.tile_pool(name="outs", bufs=12))
         psum_scalar = ctx.enter_context(tc.psum_pool(name="psum_scalar", bufs=5))
@@ -77,14 +80,27 @@ def tile_dummytemodel_pa_t_kernel(tc, hf, g1_w, g1_b, g2_w, g2_b, out):
                     in_=w1_view[g, :, c, 2 * u * HIDDEN : 2 * (u + 1) * HIDDEN],
                 )
 
-        for g in range(GROUPS):
-            load_x(CHUNKS_PER_GROUP * g)
-            for c in range(PASSES_2):
-                load_w1(g, c)
-                if (g, c) == BIAS2_BEHIND:
-                    nc.sync.dma_start(out=b2_all[:], in_=g2_b.rearrange("g h -> (g h)").partition_broadcast(P))
-            load_x(CHUNKS_PER_GROUP * g + 1)
+        def load_w2(g):
             nc.sync.dma_start(out=w2_sb[g][:], in_=w2_view[g])
+
+        units = []
+        for g in range(GROUPS + 1):
+            if g < GROUPS:
+                units.append(("x", CHUNKS_PER_GROUP * g))
+                units.extend([("w1", g, c) for c in range(PASSES_2)])
+            if g > 0:
+                units.extend([("w2", g - 1, c) for c in range(PASSES_2)])
+            if g < GROUPS:
+                units.append(("x", CHUNKS_PER_GROUP * g + 1))
+        for key in units:
+            if key[0] == "x":
+                load_x(key[1])
+            elif key[0] == "w1":
+                load_w1(key[1], key[2])
+            elif key[2] == 0:
+                load_w2(key[1])
+            if key == BIAS2_BEHIND:
+                nc.sync.dma_start(out=b2_all[:], in_=g2_b.rearrange("g h -> (g h)").partition_broadcast(P))
 
         ident = const.tile([P, P], F32)
         make_identity(nc, ident[:])
@@ -93,7 +109,7 @@ def tile_dummytemodel_pa_t_kernel(tc, hf, g1_w, g1_b, g2_w, g2_b, out):
         b1_col = const.tile([P, GROUPS * INNER_TILES], F32)
 
         def transpose_bias():
-            b1_bank = psum_scalar.tile([P, BANK], F32, tag="bank")
+            b1_bank = psum_vector.tile([P, BANK], F32, tag="vector_bank", name="vector_bank")
             planes = b1_bank[:].rearrange("p (u r) -> p u r", r=P)
             for u in range(2):
                 nc.tensor.transpose(planes[:, u, :], b1_rows[:, u:WORDS:2], ident[:])
@@ -113,24 +129,32 @@ def tile_dummytemodel_pa_t_kernel(tc, hf, g1_w, g1_b, g2_w, g2_b, out):
             words = w2_sb[key[1]][:].bitcast(F32)
             return [words[:, b, WORDS * key[2] : WORDS * (key[2] + 1)] for b in range(HIDDEN // P)]
 
+        def new_bank(engine):
+            if engine == SCALAR:
+                bank = psum_scalar.tile([P, BANK], F32, tag="scalar_bank", name="scalar_bank")
+            else:
+                bank = psum_vector.tile([P, BANK], F32, tag="vector_bank", name="vector_bank")
+            return bank
+
         grouped = {}
         codes = {}
 
-        def transpose_unit(key):
+        def transpose_half(key, half, engine):
             blocks = unit_blocks(key)
-            unit_bf16 = grouped_pool.tile([P, CHUNK, PACK], BF16, tag="unit_bf16", align_bytes=64)
+            if half == 0:
+                grouped[key] = grouped_pool.tile([P, CHUNK, PACK], BF16, tag="unit_bf16", align_bytes=64, name="unit_bf16")
+            unit_bf16 = grouped[key]
             unit_words = unit_bf16[:].bitcast(F32)
-            for half in range(2):
-                bank = psum_scalar.tile([P, BANK], F32, tag="bank")
-                planes = bank[:].rearrange("p (b u r) -> p b u r", b=2, u=2)
-                for b in range(2):
-                    for u in range(2):
-                        nc.tensor.transpose(planes[:, b, u, :], blocks[2 * half + b][:, u:WORDS:2], ident[:])
-                nc.scalar.copy(
-                    out=unit_words[:, 2 * P * half : 2 * P * (half + 1), :].rearrange("p (b r) u -> p b r u", b=2),
-                    in_=planes.rearrange("p b u r -> p b r u"),
-                )
-            grouped[key] = unit_bf16
+            bank = new_bank(engine)
+            planes = bank[:].rearrange("p (b u r) -> p b u r", b=2, u=2)
+            for b in range(2):
+                for u in range(2):
+                    nc.tensor.transpose(planes[:, b, u, :], blocks[2 * half + b][:, u:WORDS:2], ident[:])
+            destination = unit_words[:, 2 * P * half : 2 * P * (half + 1), :].rearrange("p (b r) u -> p b r u", b=2)
+            if engine == SCALAR:
+                nc.scalar.copy(out=destination, in_=planes.rearrange("p b u r -> p b r u"))
+            else:
+                nc.vector.tensor_copy(out=destination, in_=planes.rearrange("p b u r -> p b r u"))
 
         def quantise(key):
             tag = key[0]
@@ -145,39 +169,40 @@ def tile_dummytemodel_pa_t_kernel(tc, hf, g1_w, g1_b, g2_w, g2_b, out):
 
         planar = {}
 
-        def layer1(s, c):
+        def layer1(s, bank_number, engine):
             g = s // CHUNKS_PER_GROUP
+            c, j = divmod(bank_number, PACK)
             x_words, x_scales = codes[("x", s)]
             w_words, w_scales = codes[("w1", g, c)]
-            y_planar = y_pool.tile([P, PACK, CHUNK], BF16, tag="y_planar")
-            for j in range(PACK):
-                acc1 = psum_scalar.tile([P, BANK], F32, tag="bank")
-                nc.tensor.matmul_mx(
-                    out=acc1[:],
-                    lhsT=w_words[:, j * P : (j + 1) * P].bitcast(FP8X4),
-                    lhsT_scale=w_scales[:, j * P : (j + 1) * P],
-                    rhs=x_words[:].bitcast(FP8X4),
-                    rhs_scale=x_scales[:],
-                    start=True,
-                    stop=True,
+            if j == 0:
+                planar[(s, c)] = y_pool.tile([P, PACK, CHUNK], BF16, tag="y_planar", name="y_planar")
+            y_planar = planar[(s, c)]
+            acc1 = new_bank(engine)
+            nc.tensor.matmul_mx(
+                out=acc1[:],
+                lhsT=w_words[:, j * P : (j + 1) * P].bitcast(FP8X4),
+                lhsT_scale=w_scales[:, j * P : (j + 1) * P],
+                rhs=x_words[:].bitcast(FP8X4),
+                rhs_scale=x_scales[:],
+                start=True,
+                stop=True,
+            )
+            column = INNER_TILES * g + bank_number
+            if engine == SCALAR:
+                nc.scalar.activation(
+                    out=y_planar[:, j, :],
+                    in_=acc1[:],
+                    func=mybir.ActivationFunctionType.Identity,
+                    bias=b1_col[:, column : column + 1],
                 )
-                column = INNER_TILES * g + PACK * c + j
-                if s < ROUNDS_WITH_HELP and j % 2 == 1:
-                    nc.vector.tensor_scalar(
-                        out=y_planar[:, j, :],
-                        in0=acc1[:],
-                        scalar1=b1_col[:, column : column + 1],
-                        scalar2=None,
-                        op0=mybir.AluOpType.add,
-                    )
-                else:
-                    nc.scalar.activation(
-                        out=y_planar[:, j, :],
-                        in_=acc1[:],
-                        func=mybir.ActivationFunctionType.Identity,
-                        bias=b1_col[:, column : column + 1],
-                    )
-            planar[(s, c)] = y_planar
+            else:
+                nc.vector.tensor_scalar(
+                    out=y_planar[:, j, :],
+                    in0=acc1[:],
+                    scalar1=b1_col[:, column : column + 1],
+                    scalar2=None,
+                    op0=mybir.AluOpType.add,
+                )
 
         def regroup_y(s, c):
             y_bf16 = y_pool.tile([P, CHUNK, PACK], BF16, tag="y_bf16", align_bytes=64)
@@ -189,7 +214,7 @@ def tile_dummytemodel_pa_t_kernel(tc, hf, g1_w, g1_b, g2_w, g2_b, out):
 
         def layer2(s, b):
             g, n = divmod(s, CHUNKS_PER_GROUP)
-            acc2 = psum_vector.tile([P, HIDDEN], F32, tag="acc2")
+            acc2 = new_bank(VECTOR)
             for c in range(PASSES_2):
                 y_words, y_scales = codes[("y", s, c)]
                 w_words, w_scales = codes[("w2", g, c)]
@@ -211,51 +236,49 @@ def tile_dummytemodel_pa_t_kernel(tc, hf, g1_w, g1_b, g2_w, g2_b, out):
             )
             nc.sync.dma_start(out=out_view[g, :, n * BLOCKS + b, :], in_=result[:])
 
-        units = []
-        for g in range(GROUPS):
-            units.append(("x", CHUNKS_PER_GROUP * g))
-            units.extend([("w1", g, c) for c in range(PASSES_2)])
-            units.append(("x", CHUNKS_PER_GROUP * g + 1))
-            units.extend([("w2", g, c) for c in range(PASSES_2)])
+        halves = [(key, half) for key in units for half in range(2)]
+        progress = {"halves": 0, "quantised": 0}
+
+        def transpose_next(engine=SCALAR):
+            if progress["halves"] < len(halves):
+                key, half = halves[progress["halves"]]
+                transpose_half(key, half, engine)
+                progress["halves"] += 1
+
+        def quantise_next():
+            if 2 * progress["quantised"] < progress["halves"]:
+                quantise(units[progress["quantised"]])
+                progress["quantised"] += 1
 
         for i in range(LEAD):
-            transpose_unit(units[i])
+            transpose_next()
+            transpose_next(VECTOR if i == 1 else SCALAR)
             if i == 0:
                 transpose_bias()
             else:
-                quantise(units[i - 1])
-        quantise(units[LEAD - 1])
+                quantise_next()
+        quantise_next()
 
-        for s in range(CHUNKS + 1):
-            first = LEAD + UNITS_PER_ROUND * s
-            unit_a, unit_b, unit_c = units[first : first + 1], units[first + 1 : first + 2], units[first + 2 : first + 3]
-            here, behind = s < CHUNKS, s > 0
-            if here:
-                layer1(s, 0)
-            for key in unit_a:
-                transpose_unit(key)
-            if behind:
-                layer2(s - 1, 0)
-            if here:
-                regroup_y(s, 0)
-            for key in unit_a:
-                quantise(key)
-            if here:
-                layer1(s, 1)
-            if behind:
-                layer2(s - 1, 1)
-            if here:
-                quantise(("y", s, 0))
-            for key in unit_b + unit_c:
-                transpose_unit(key)
-            if here:
-                regroup_y(s, 1)
-            for key in unit_b:
-                quantise(key)
-            if here:
-                quantise(("y", s, 1))
-            for key in unit_c:
-                quantise(key)
-            if behind:
-                layer2(s - 1, 2)
-                layer2(s - 1, 3)
+        for s in range(CHUNKS + LAG):
+            here, behind = s < CHUNKS, s >= LAG
+            for quarter in range(QUARTERS):
+                if here:
+                    layer1(s, 2 * quarter, SCALAR)
+                    layer1(s, 2 * quarter + 1, VECTOR if not behind and quarter % 2 == 1 else SCALAR)
+                if behind:
+                    layer2(s - LAG, quarter)
+                if quarter == 0 and 0 < s <= CHUNKS:
+                    quantise(("y", s - 1, 1))
+                if quarter == 1:
+                    quantise_next()
+                if quarter == 2 and here:
+                    regroup_y(s, 0)
+                if quarter == 3 and here:
+                    regroup_y(s, 1)
+            for i in range(UNITS_PER_ROUND):
+                transpose_next()
+                transpose_next()
+                if i < 2:
+                    quantise_next()
+                elif here:
+                    quantise(("y", s, 0))

@@ -25,10 +25,11 @@ PASSES_2 = INNER // K_PASS
 INNER_TILES = INNER // P
 
 LEAD = 4
-UNITS_PER_ROUND = 3
-LAG = 2
-QUARTERS = 4
+HALVES_PER_ROUND = 3
+LAG = 3
 BIAS2_BEHIND = ("w1", 1, 0)
+
+WARM_UP = 4
 
 SCALAR, VECTOR = "scalar", "vector"
 
@@ -47,6 +48,15 @@ def tile_dummytemodel_pa_t_kernel(tc, hf, g1_w, g1_b, g2_w, g2_b, out):
         psum_scalar = ctx.enter_context(tc.psum_pool(name="psum_scalar", bufs=5))
         psum_vector = ctx.enter_context(tc.psum_pool(name="psum_vector", bufs=3))
         ctx.enter_context(tc.manual_schedule())
+
+        idle = const.tile([P, P * 2], F32)
+        nc.gpsimd.memset(idle[:], 0.0)
+        idle_bf16 = idle[:].bitcast(BF16)
+
+        def keep_warm(times, columns):
+            unused = psum_vector.tile([P, BANK], F32, tag="vector_bank", name="vector_bank")
+            for turn in range(times):
+                nc.tensor.matmul(out=unused[:, 0:columns], lhsT=idle_bf16[:, 0:P], rhs=idle_bf16[:, 0:columns], start=True, stop=True)
 
         hf_view = hf.rearrange("(g r a) k -> g r a k", g=GROUPS, r=P)
         out_view = out.rearrange("(g r a) h -> g r a h", g=GROUPS, r=P)
@@ -84,14 +94,11 @@ def tile_dummytemodel_pa_t_kernel(tc, hf, g1_w, g1_b, g2_w, g2_b, out):
             nc.sync.dma_start(out=w2_sb[g][:], in_=w2_view[g])
 
         units = []
-        for g in range(GROUPS + 1):
-            if g < GROUPS:
-                units.append(("x", CHUNKS_PER_GROUP * g))
-                units.extend([("w1", g, c) for c in range(PASSES_2)])
-            if g > 0:
-                units.extend([("w2", g - 1, c) for c in range(PASSES_2)])
-            if g < GROUPS:
-                units.append(("x", CHUNKS_PER_GROUP * g + 1))
+        for g in range(GROUPS):
+            units.append(("x", CHUNKS_PER_GROUP * g))
+            units.extend([("w1", g, c) for c in range(PASSES_2)])
+            units.append(("x", CHUNKS_PER_GROUP * g + 1))
+            units.extend([("w2", g, c) for c in range(PASSES_2)])
         for key in units:
             if key[0] == "x":
                 load_x(key[1])
@@ -206,10 +213,13 @@ def tile_dummytemodel_pa_t_kernel(tc, hf, g1_w, g1_b, g2_w, g2_b, out):
 
         def regroup_y(s, c):
             y_bf16 = y_pool.tile([P, CHUNK, PACK], BF16, tag="y_bf16", align_bytes=64)
-            nc.vector.tensor_copy(
-                out=y_bf16[:].rearrange("p (t i) j -> p t j i", i=4),
-                in_=planar[(s, c)][:].rearrange("p j (t i) -> p t j i", i=4),
-            )
+            regrouped = y_bf16[:].rearrange("p (t i) j -> p t j i", i=4)
+            source = planar[(s, c)][:].rearrange("p j (t i) -> p t j i", i=4)
+            if (s, c) == (CHUNKS - 1, PASSES_2 - 1):
+                cut = CHUNK // 4 // 2
+                nc.scalar.copy(out=regrouped[:, cut:, :, :], in_=source[:, cut:, :, :])
+                regrouped, source = regrouped[:, 0:cut, :, :], source[:, 0:cut, :, :]
+            nc.vector.tensor_copy(out=regrouped, in_=source)
             grouped[("y", s, c)] = y_bf16
 
         def layer2(s, b):
@@ -246,39 +256,38 @@ def tile_dummytemodel_pa_t_kernel(tc, hf, g1_w, g1_b, g2_w, g2_b, out):
                 progress["halves"] += 1
 
         def quantise_next():
-            if 2 * progress["quantised"] < progress["halves"]:
+            if 2 * progress["quantised"] + 2 <= progress["halves"]:
                 quantise(units[progress["quantised"]])
                 progress["quantised"] += 1
 
+        keep_warm(WARM_UP, BANK)
         for i in range(LEAD):
             transpose_next()
+            if i > 0:
+                quantise_next()
             transpose_next(VECTOR if i == 1 else SCALAR)
+            keep_warm(1, BANK // 2)
             if i == 0:
                 transpose_bias()
-            else:
-                quantise_next()
         quantise_next()
 
-        for s in range(CHUNKS + LAG):
-            here, behind = s < CHUNKS, s >= LAG
-            for quarter in range(QUARTERS):
+        rounds = CHUNKS * PASSES_2
+        for n in range(rounds + LAG):
+            s, c = divmod(n, PASSES_2)
+            here, behind = n < rounds, n >= LAG
+            for pair in range(2):
                 if here:
-                    layer1(s, 2 * quarter, SCALAR)
-                    layer1(s, 2 * quarter + 1, VECTOR if not behind and quarter % 2 == 1 else SCALAR)
+                    layer1(s, PACK * c + 2 * pair, SCALAR)
+                    layer1(s, PACK * c + 2 * pair + 1, VECTOR if not behind and pair == 1 else SCALAR)
                 if behind:
-                    layer2(s - LAG, quarter)
-                if quarter == 0 and 0 < s <= CHUNKS:
-                    quantise(("y", s - 1, 1))
-                if quarter == 1:
-                    quantise_next()
-                if quarter == 2 and here:
-                    regroup_y(s, 0)
-                if quarter == 3 and here:
-                    regroup_y(s, 1)
-            for i in range(UNITS_PER_ROUND):
+                    earlier, half = divmod(n - LAG, 2)
+                    layer2(earlier, 2 * half + pair)
+            for i in range(HALVES_PER_ROUND):
                 transpose_next()
-                transpose_next()
-                if i < 2:
-                    quantise_next()
-                elif here:
-                    quantise(("y", s, 0))
+            if here:
+                regroup_y(s, c)
+            quantise_next()
+            if here:
+                quantise(("y", s, c))
+            if c == 1:
+                quantise_next()

@@ -45,6 +45,7 @@ def tile_dummytemodel_pa_t_kernel(tc, hf, g1_w, g1_b, g2_w, g2_b, out):
         codes_pool = ctx.enter_context(tc.tile_pool(name="codes", bufs=6))
         y_pool = ctx.enter_context(tc.tile_pool(name="y", bufs=3))
         out_pool = ctx.enter_context(tc.tile_pool(name="outs", bufs=12))
+        product_pool = ctx.enter_context(tc.tile_pool(name="products", bufs=2))
         psum_scalar = ctx.enter_context(tc.psum_pool(name="psum_scalar", bufs=5))
         psum_vector = ctx.enter_context(tc.psum_pool(name="psum_vector", bufs=3))
         ctx.enter_context(tc.manual_schedule())
@@ -163,16 +164,18 @@ def tile_dummytemodel_pa_t_kernel(tc, hf, g1_w, g1_b, g2_w, g2_b, out):
             else:
                 nc.vector.tensor_copy(out=destination, in_=planes.rearrange("p b u r -> p b r u"))
 
-        def quantise(key):
-            tag = key[0]
-            words = codes_pool.tile([P, CHUNK], U32, tag=tag + "_words", align_bytes=64)
-            scales = codes_pool.tile([P, CHUNK], U8, tag=tag + "_scales", align_bytes=64)
+        def quantise(key, first=0, last=CHUNK):
+            if first == 0:
+                tag = key[0]
+                words = codes_pool.tile([P, CHUNK], U32, tag=tag + "_words", align_bytes=64)
+                scales = codes_pool.tile([P, CHUNK], U8, tag=tag + "_scales", align_bytes=64)
+                codes[key] = (words, scales)
+            words, scales = codes[key]
             nc.vector.quantize_mx(
-                out=words[:].bitcast(FP8X4),
-                scales=scales[:],
-                in_=grouped[key][:].rearrange("p c j -> p (c j)"),
+                out=words[:, first:last].bitcast(FP8X4),
+                scales=scales[:, first:last],
+                in_=grouped[key][:, first:last, :].rearrange("p c j -> p (c j)"),
             )
-            codes[key] = (words, scales)
 
         planar = {}
 
@@ -211,40 +214,55 @@ def tile_dummytemodel_pa_t_kernel(tc, hf, g1_w, g1_b, g2_w, g2_b, out):
                     op0=mybir.AluOpType.add,
                 )
 
-        def regroup_y(s, c):
+        def regroup_y(s, c, shared=False):
             y_bf16 = y_pool.tile([P, CHUNK, PACK], BF16, tag="y_bf16", align_bytes=64)
             regrouped = y_bf16[:].rearrange("p (t i) j -> p t j i", i=4)
             source = planar[(s, c)][:].rearrange("p j (t i) -> p t j i", i=4)
-            if (s, c) == (CHUNKS - 1, PASSES_2 - 1):
+            if shared:
                 cut = CHUNK // 4 // 2
+                nc.vector.tensor_copy(out=regrouped[:, 0:cut, :, :], in_=source[:, 0:cut, :, :])
                 nc.scalar.copy(out=regrouped[:, cut:, :, :], in_=source[:, cut:, :, :])
-                regrouped, source = regrouped[:, 0:cut, :, :], source[:, 0:cut, :, :]
-            nc.vector.tensor_copy(out=regrouped, in_=source)
+            else:
+                nc.vector.tensor_copy(out=regrouped, in_=source)
             grouped[("y", s, c)] = y_bf16
 
-        def layer2(s, b):
-            g, n = divmod(s, CHUNKS_PER_GROUP)
-            acc2 = new_bank(VECTOR)
-            for c in range(PASSES_2):
-                y_words, y_scales = codes[("y", s, c)]
-                w_words, w_scales = codes[("w2", g, c)]
-                nc.tensor.matmul_mx(
-                    out=acc2[:],
-                    lhsT=y_words[:, b * P : (b + 1) * P].bitcast(FP8X4),
-                    lhsT_scale=y_scales[:, b * P : (b + 1) * P],
-                    rhs=w_words[:].bitcast(FP8X4),
-                    rhs_scale=w_scales[:],
-                    start=(c == 0),
-                    stop=(c == PASSES_2 - 1),
-                )
-            result = out_pool.tile([P, HIDDEN], F32, tag="result")
-            nc.vector.tensor_tensor(
-                out=result[:],
-                in0=acc2[:],
-                in1=b2_all[:, g * HIDDEN : (g + 1) * HIDDEN],
-                op=mybir.AluOpType.add,
+        def layer2_pass(s, b, c, acc2):
+            g = s // CHUNKS_PER_GROUP
+            y_words, y_scales = codes[("y", s, c)]
+            w_words, w_scales = codes[("w2", g, c)]
+            nc.tensor.matmul_mx(
+                out=acc2[:],
+                lhsT=y_words[:, b * P : (b + 1) * P].bitcast(FP8X4),
+                lhsT_scale=y_scales[:, b * P : (b + 1) * P],
+                rhs=w_words[:].bitcast(FP8X4),
+                rhs_scale=w_scales[:],
+                start=(c == 0),
+                stop=(c == PASSES_2 - 1),
             )
-            nc.sync.dma_start(out=out_view[g, :, n * BLOCKS + b, :], in_=result[:])
+
+        def add_bias2(s, acc2, engine, columns=slice(0, HIDDEN)):
+            g = s // CHUNKS_PER_GROUP
+            bias = b2_all[:, g * HIDDEN : (g + 1) * HIDDEN][:, columns]
+            acc2 = acc2[:, columns]
+            width = columns.stop - columns.start
+            result = out_pool.tile([P, width], F32, tag="result", name="result")
+            if engine == VECTOR:
+                nc.vector.tensor_tensor(out=result[:], in0=acc2, in1=bias, op=mybir.AluOpType.add)
+            else:
+                product = product_pool.tile([P, width], F32, tag="product", name="product")
+                nc.scalar.copy(out=product[:], in_=acc2)
+                nc.gpsimd.tensor_tensor(out=result[:], in0=product[:], in1=bias, op=mybir.AluOpType.add)
+            return result
+
+        def store(s, b, result, columns=slice(0, HIDDEN)):
+            g, n = divmod(s, CHUNKS_PER_GROUP)
+            nc.sync.dma_start(out=out_view[g, :, n * BLOCKS + b, columns], in_=result[:])
+
+        def layer2(s, b, engine=VECTOR):
+            acc2 = new_bank(engine)
+            for c in range(PASSES_2):
+                layer2_pass(s, b, c, acc2)
+            return add_bias2(s, acc2, engine)
 
         halves = [(key, half) for key in units for half in range(2)]
         progress = {"halves": 0, "quantised": 0}
@@ -267,27 +285,53 @@ def tile_dummytemodel_pa_t_kernel(tc, hf, g1_w, g1_b, g2_w, g2_b, out):
                 quantise_next()
             transpose_next(VECTOR if i == 1 else SCALAR)
             keep_warm(1, BANK // 2)
-            if i == 0:
+            if i == 2:
                 transpose_bias()
         quantise_next()
 
         rounds = CHUNKS * PASSES_2
-        for n in range(rounds + LAG):
+        for n in range(rounds - 1):
             s, c = divmod(n, PASSES_2)
-            here, behind = n < rounds, n >= LAG
+            behind = n >= LAG
             for pair in range(2):
-                if here:
-                    layer1(s, PACK * c + 2 * pair, SCALAR)
-                    layer1(s, PACK * c + 2 * pair + 1, VECTOR if not behind and pair == 1 else SCALAR)
+                layer1(s, PACK * c + 2 * pair, SCALAR)
+                layer1(s, PACK * c + 2 * pair + 1, VECTOR if not behind and pair == 1 else SCALAR)
                 if behind:
                     earlier, half = divmod(n - LAG, 2)
-                    layer2(earlier, 2 * half + pair)
+                    store(earlier, 2 * half + pair, layer2(earlier, 2 * half + pair))
             for i in range(HALVES_PER_ROUND):
                 transpose_next()
-            if here:
-                regroup_y(s, c)
+            regroup_y(s, c)
             quantise_next()
-            if here:
+            if n < rounds - 2:
                 quantise(("y", s, c))
             if c == 1:
                 quantise_next()
+
+        last, before = CHUNKS - 1, CHUNKS - 2
+        for pair in range(2):
+            layer1(last, PACK + 2 * pair, SCALAR)
+            layer1(last, PACK + 2 * pair + 1, SCALAR)
+            if pair == 0:
+                store(before, 0, layer2(before, 0))
+                quantise(("y", last, 0))
+        regroup_y(last, 1, shared=True)
+        store(before, 1, layer2(before, 1))
+        quantise(("y", last, 1), 0, CHUNK // 2)
+        store(before, 2, layer2(before, 2))
+        result3 = layer2(before, 3, SCALAR)
+        accs = [new_bank(VECTOR if b == 0 else SCALAR) for b in range(BLOCKS)]
+        for b in range(BLOCKS):
+            layer2_pass(last, b, 0, accs[b])
+        for b in range(BLOCKS):
+            layer2_pass(last, b, 1, accs[b])
+            if b < BLOCKS - 1:
+                store(last, b, add_bias2(last, accs[b], VECTOR))
+            else:
+                for half in range(2):
+                    columns = slice(half * HIDDEN // 2, (half + 1) * HIDDEN // 2)
+                    store(last, b, add_bias2(last, accs[b], VECTOR, columns), columns)
+            if b == 0:
+                quantise(("y", last, 1), CHUNK // 2, CHUNK)
+            if b == 1:
+                store(before, 3, result3)

@@ -179,52 +179,62 @@ def tile_dummytemodel_pa_t_kernel(tc, hf, g1_w, g1_b, g2_w, g2_b, out):
 
         planar = {}
 
-        def layer1(s, bank_number, engine):
-            g = s // CHUNKS_PER_GROUP
-            c, j = divmod(bank_number, PACK)
+        def layer1_pass(s, c, j, tokens, out):
             x_words, x_scales = codes[("x", s)]
-            w_words, w_scales = codes[("w1", g, c)]
-            if j == 0:
-                planar[(s, c)] = y_pool.tile([P, PACK, CHUNK], BF16, tag="y_planar", name="y_planar")
-            y_planar = planar[(s, c)]
-            acc1 = new_bank(engine)
+            w_words, w_scales = codes[("w1", s // CHUNKS_PER_GROUP, c)]
             nc.tensor.matmul_mx(
-                out=acc1[:],
+                out=out,
                 lhsT=w_words[:, j * P : (j + 1) * P].bitcast(FP8X4),
                 lhsT_scale=w_scales[:, j * P : (j + 1) * P],
-                rhs=x_words[:].bitcast(FP8X4),
-                rhs_scale=x_scales[:],
+                rhs=x_words[:, tokens].bitcast(FP8X4),
+                rhs_scale=x_scales[:, tokens],
                 start=True,
                 stop=True,
             )
-            column = INNER_TILES * g + bank_number
-            if engine == SCALAR:
-                nc.scalar.activation(
-                    out=y_planar[:, j, :],
-                    in_=acc1[:],
-                    func=mybir.ActivationFunctionType.Identity,
-                    bias=b1_col[:, column : column + 1],
-                )
-            else:
-                nc.vector.tensor_scalar(
-                    out=y_planar[:, j, :],
-                    in0=acc1[:],
-                    scalar1=b1_col[:, column : column + 1],
-                    scalar2=None,
-                    op0=mybir.AluOpType.add,
-                )
 
-        def regroup_y(s, c, shared=False):
-            y_bf16 = y_pool.tile([P, CHUNK, PACK], BF16, tag="y_bf16", align_bytes=64)
-            regrouped = y_bf16[:].rearrange("p (t i) j -> p t j i", i=4)
+        def bias1(s, c):
+            first = INNER_TILES * (s // CHUNKS_PER_GROUP) + PACK * c
+            return b1_col[:, first : first + PACK]
+
+        def layer1_scalar(s, c, j, tokens):
+            if j == 0:
+                planar[(s, c)] = y_pool.tile([P, PACK, CHUNK], BF16, tag="y_planar", name="y_planar")
+            acc1 = new_bank(SCALAR)
+            width = tokens.stop - tokens.start
+            layer1_pass(s, c, j, tokens, acc1[:, 0:width])
+            nc.scalar.activation(
+                out=planar[(s, c)][:, j, tokens],
+                in_=acc1[:, 0:width],
+                func=mybir.ActivationFunctionType.Identity,
+                bias=bias1(s, c)[:, j : j + 1],
+            )
+
+        def layer1_vector(s, c, tokens):
+            acc1 = new_bank(VECTOR)
+            tiles = acc1[:].rearrange("p (j t) -> p j t", j=PACK)
+            for j in range(PACK):
+                layer1_pass(s, c, j, tokens, tiles[:, j, :])
+            nc.vector.tensor_tensor(
+                out=word_order(s, c)[:, tokens, :],
+                in0=tiles.rearrange("p j t -> p t j"),
+                in1=bias1(s, c).unsqueeze(1).to_broadcast([P, P, PACK]),
+                op=mybir.AluOpType.add,
+            )
+
+        def word_order(s, c):
+            if ("y", s, c) not in grouped:
+                y_bf16 = y_pool.tile([P, CHUNK, PACK], BF16, tag="y_bf16", align_bytes=64, name="y_bf16")
+                grouped[("y", s, c)] = y_bf16
+            return grouped[("y", s, c)]
+
+        def regroup_y(s, c, last_token=CHUNK, shared=False):
+            regrouped = word_order(s, c)[:].rearrange("p (t i) j -> p t j i", i=4)
             source = planar[(s, c)][:].rearrange("p j (t i) -> p t j i", i=4)
+            end = last_token // 4
             if shared:
-                cut = CHUNK // 4 // 2
-                nc.vector.tensor_copy(out=regrouped[:, 0:cut, :, :], in_=source[:, 0:cut, :, :])
-                nc.scalar.copy(out=regrouped[:, cut:, :, :], in_=source[:, cut:, :, :])
-            else:
-                nc.vector.tensor_copy(out=regrouped, in_=source)
-            grouped[("y", s, c)] = y_bf16
+                nc.scalar.copy(out=regrouped[:, end // 2 : end, :, :], in_=source[:, end // 2 : end, :, :])
+                end = end // 2
+            nc.vector.tensor_copy(out=regrouped[:, 0:end, :, :], in_=source[:, 0:end, :, :])
 
         def layer2_pass(s, b, c, acc2):
             g = s // CHUNKS_PER_GROUP
@@ -290,18 +300,22 @@ def tile_dummytemodel_pa_t_kernel(tc, hf, g1_w, g1_b, g2_w, g2_b, out):
         quantise_next()
 
         rounds = CHUNKS * PASSES_2
+        every_token = slice(0, CHUNK)
         for n in range(rounds - 1):
             s, c = divmod(n, PASSES_2)
             behind = n >= LAG
+            scalar_tokens = every_token if behind else slice(0, CHUNK // 2)
             for pair in range(2):
-                layer1(s, PACK * c + 2 * pair, SCALAR)
-                layer1(s, PACK * c + 2 * pair + 1, VECTOR if not behind and pair == 1 else SCALAR)
+                layer1_scalar(s, c, 2 * pair, scalar_tokens)
+                layer1_scalar(s, c, 2 * pair + 1, scalar_tokens)
                 if behind:
                     earlier, half = divmod(n - LAG, 2)
                     store(earlier, 2 * half + pair, layer2(earlier, 2 * half + pair))
+                else:
+                    layer1_vector(s, c, slice((2 + pair) * P, (3 + pair) * P))
             for i in range(HALVES_PER_ROUND):
                 transpose_next()
-            regroup_y(s, c)
+            regroup_y(s, c, scalar_tokens.stop)
             quantise_next()
             if n < rounds - 2:
                 quantise(("y", s, c))
@@ -310,8 +324,8 @@ def tile_dummytemodel_pa_t_kernel(tc, hf, g1_w, g1_b, g2_w, g2_b, out):
 
         last, before = CHUNKS - 1, CHUNKS - 2
         for pair in range(2):
-            layer1(last, PACK + 2 * pair, SCALAR)
-            layer1(last, PACK + 2 * pair + 1, SCALAR)
+            layer1_scalar(last, 1, 2 * pair, every_token)
+            layer1_scalar(last, 1, 2 * pair + 1, every_token)
             if pair == 0:
                 store(before, 0, layer2(before, 0))
                 quantise(("y", last, 0))

@@ -107,8 +107,11 @@ def tile_dummytemodel_pa_t_kernel(tc, hf, g1_w, g1_b, g2_w, g2_b, out):
                 load_w1(key[1], key[2])
             elif key[2] == 0:
                 load_w2(key[1])
-            if key == BIAS2_BEHIND:
-                nc.sync.dma_start(out=b2_all[:], in_=g2_b.rearrange("g h -> (g h)").partition_broadcast(P))
+                columns = slice(key[1] * HIDDEN, (key[1] + 1) * HIDDEN)
+                nc.sync.dma_start(
+                    out=b2_all[:, columns],
+                    in_=g2_b.rearrange("g h -> (g h)")[columns].partition_broadcast(P),
+                )
 
         ident = const.tile([P, P], F32)
         make_identity(nc, ident[:])
@@ -232,9 +235,10 @@ def tile_dummytemodel_pa_t_kernel(tc, hf, g1_w, g1_b, g2_w, g2_b, out):
             source = planar[(s, c)][:].rearrange("p j (t i) -> p t j i", i=4)
             end = last_token // 4
             if shared:
-                nc.scalar.copy(out=regrouped[:, end // 2 : end, :, :], in_=source[:, end // 2 : end, :, :])
-                end = end // 2
-            nc.vector.tensor_copy(out=regrouped[:, 0:end, :, :], in_=source[:, 0:end, :, :])
+                for first, last in ((0, end // 2), (end // 2, end)):
+                    nc.scalar.copy(out=regrouped[:, first:last, :, :], in_=source[:, first:last, :, :])
+            else:
+                nc.vector.tensor_copy(out=regrouped[:, 0:end, :, :], in_=source[:, 0:end, :, :])
 
         def layer2_pass(s, b, c, acc2):
             g = s // CHUNKS_PER_GROUP
@@ -331,21 +335,18 @@ def tile_dummytemodel_pa_t_kernel(tc, hf, g1_w, g1_b, g2_w, g2_b, out):
                 quantise(("y", last, 0))
         regroup_y(last, 1, shared=True)
         store(before, 1, layer2(before, 1))
-        quantise(("y", last, 1), 0, CHUNK // 2)
         store(before, 2, layer2(before, 2))
-        result3 = layer2(before, 3, SCALAR)
-        accs = [new_bank(VECTOR if b == 0 else SCALAR) for b in range(BLOCKS)]
+        quantise(("y", last, 1), 0, CHUNK // 2)
+        store(before, 3, layer2(before, 3))
+        quantise(("y", last, 1), CHUNK // 2, CHUNK)
+        accs = [new_bank(SCALAR) for b in range(BLOCKS)]
+        for c in range(PASSES_2):
+            for b in range(BLOCKS):
+                layer2_pass(last, b, c, accs[b])
         for b in range(BLOCKS):
-            layer2_pass(last, b, 0, accs[b])
-        for b in range(BLOCKS):
-            layer2_pass(last, b, 1, accs[b])
             if b < BLOCKS - 1:
                 store(last, b, add_bias2(last, accs[b], VECTOR))
             else:
                 for half in range(2):
                     columns = slice(half * HIDDEN // 2, (half + 1) * HIDDEN // 2)
                     store(last, b, add_bias2(last, accs[b], VECTOR, columns), columns)
-            if b == 0:
-                quantise(("y", last, 1), CHUNK // 2, CHUNK)
-            if b == 1:
-                store(before, 3, result3)

from contextlib import ExitStack

import concourse.mybir as mybir
from concourse.masks import make_identity

F32 = mybir.dt.float32
BF16 = mybir.dt.bfloat16
U32 = mybir.dt.uint32
U8 = mybir.dt.uint8
FP8X4 = mybir.dt.float8_e4m3fn_x4

P = 128
PACK = 4
K_PASS = P * PACK
WORDS = K_PASS // 2
BANK = 512

GROUPS, TOKENS, HIDDEN, INNER = 4, 4096, 512, 1024
GROUP_TOKENS = TOKENS // GROUPS
CHUNK = 512
CHUNKS = TOKENS // CHUNK
CHUNKS_PER_GROUP = GROUP_TOKENS // CHUNK
BLOCKS = CHUNK // P
PASSES_2 = INNER // K_PASS
INNER_TILES = INNER // P

LEAD = 4
HALVES_PER_ROUND = 3
LAG = 3
BIAS2_BEHIND = ("w1", 1, 0)

WARM_UP = 4

SCALAR, VECTOR = "scalar", "vector"

FLOPS = 2 * TOKENS * HIDDEN * INNER * 2


def tile_dummytemodel_pa_t_kernel(tc, hf, g1_w, g1_b, g2_w, g2_b, out):
    nc = tc.nc
    with ExitStack() as ctx:
        const = ctx.enter_context(tc.tile_pool(name="const", bufs=1))
        inputs = ctx.enter_context(tc.tile_pool(name="inputs", bufs=1))
        grouped_pool = ctx.enter_context(tc.tile_pool(name="grouped", bufs=4))
        codes_pool = ctx.enter_context(tc.tile_pool(name="codes", bufs=6))
        y_pool = ctx.enter_context(tc.tile_pool(name="y", bufs=3))
        out_pool = ctx.enter_context(tc.tile_pool(name="outs", bufs=12))
        product_pool = ctx.enter_context(tc.tile_pool(name="products", bufs=2))
        psum_scalar = ctx.enter_context(tc.psum_pool(name="psum_scalar", bufs=5))
        psum_vector = ctx.enter_context(tc.psum_pool(name="psum_vector", bufs=3))
        ctx.enter_context(tc.manual_schedule())

        idle = const.tile([P, P * 2], F32)
        nc.gpsimd.memset(idle[:], 0.0)
        idle_bf16 = idle[:].bitcast(BF16)

        def keep_warm(times, columns):
            unused = psum_vector.tile([P, BANK], F32, tag="vector_bank", name="vector_bank")
            for turn in range(times):
                nc.tensor.matmul(out=unused[:, 0:columns], lhsT=idle_bf16[:, 0:P], rhs=idle_bf16[:, 0:columns], start=True, stop=True)

        hf_view = hf.rearrange("(g r a) k -> g r a k", g=GROUPS, r=P)
        out_view = out.rearrange("(g r a) h -> g r a h", g=GROUPS, r=P)
        w1_view = g1_w.rearrange("g (c r t) k -> g r c (t k)", r=P, t=PACK)
        w2_view = g2_w.rearrange("g (b r) i -> g r b i", r=P)

        x_sb = [inputs.tile([P, BLOCKS, HIDDEN], BF16, name="x_sb%d" % s) for s in range(CHUNKS)]
        w1_sb = [inputs.tile([P, INNER_TILES, HIDDEN], BF16, name="w1_sb%d" % g) for g in range(GROUPS)]
        w2_sb = [inputs.tile([P, HIDDEN // P, INNER], BF16, name="w2_sb%d" % g) for g in range(GROUPS)]

        b1_rows = const.tile([P, WORDS], F32)
        nc.vector.memset(b1_rows[:], 0.0)
        nc.scalar.dma_start(
            out=b1_rows[:].bitcast(BF16)[0 : GROUPS * PASSES_2, :],
            in_=g1_b.rearrange("g (c w) -> (g c) w", w=K_PASS),
        )
        b2_all = const.tile([P, GROUPS * HIDDEN], BF16)

        def load_x(s):
            g, n = divmod(s, CHUNKS_PER_GROUP)
            for half in range(2):
                nc.sync.dma_start(
                    out=x_sb[s][:, 2 * half : 2 * half + 2, :],
                    in_=hf_view[g, :, n * BLOCKS + 2 * half : n * BLOCKS + 2 * half + 2, :],
                )

        def load_w1(g, c):
            for u in range(2):
                nc.sync.dma_start(
                    out=w1_sb[g][:, PACK * c + 2 * u : PACK * c + 2 * u + 2, :].rearrange("p e k -> p (e k)"),
                    in_=w1_view[g, :, c, 2 * u * HIDDEN : 2 * (u + 1) * HIDDEN],
                )

        def load_w2(g):
            nc.sync.dma_start(out=w2_sb[g][:], in_=w2_view[g])

        units = []
        for g in range(GROUPS):
            units.append(("x", CHUNKS_PER_GROUP * g))
            units.extend([("w1", g, c) for c in range(PASSES_2)])
            units.append(("x", CHUNKS_PER_GROUP * g + 1))
            units.extend([("w2", g, c) for c in range(PASSES_2)])
        for key in units:
            if key[0] == "x":
                load_x(key[1])
            elif key[0] == "w1":
                load_w1(key[1], key[2])
            elif key[2] == 0:
                load_w2(key[1])
                columns = slice(key[1] * HIDDEN, (key[1] + 1) * HIDDEN)
                nc.sync.dma_start(
                    out=b2_all[:, columns],
                    in_=g2_b.rearrange("g h -> (g h)")[columns].partition_broadcast(P),
                )

        ident = const.tile([P, P], F32)
        make_identity(nc, ident[:])

        b1_words = const.tile([P, GROUPS * PASSES_2, 2], F32)
        b1_col = const.tile([P, GROUPS * INNER_TILES], F32)

        def transpose_bias():
            b1_bank = psum_vector.tile([P, BANK], F32, tag="vector_bank", name="vector_bank")
            planes = b1_bank[:].rearrange("p (u r) -> p u r", r=P)
            for u in range(2):
                nc.tensor.transpose(planes[:, u, :], b1_rows[:, u:WORDS:2], ident[:])
            nc.vector.tensor_copy(
                out=b1_words[:], in_=planes[:, 0:2, 0 : GROUPS * PASSES_2].rearrange("p u r -> p r u")
            )
            nc.vector.tensor_copy(out=b1_col[:], in_=b1_words[:].rearrange("p r u -> p (r u)").bitcast(BF16))

        def unit_blocks(key):
            kind = key[0]
            if kind == "x":
                words = x_sb[key[1]][:].bitcast(F32)
                return [words[:, a, :] for a in range(BLOCKS)]
            if kind == "w1":
                words = w1_sb[key[1]][:].bitcast(F32)
                return [words[:, PACK * key[2] + j, :] for j in range(PACK)]
            words = w2_sb[key[1]][:].bitcast(F32)
            return [words[:, b, WORDS * key[2] : WORDS * (key[2] + 1)] for b in range(HIDDEN // P)]

        def new_bank(engine):
            if engine == SCALAR:
                bank = psum_scalar.tile([P, BANK], F32, tag="scalar_bank", name="scalar_bank")
            else:
                bank = psum_vector.tile([P, BANK], F32, tag="vector_bank", name="vector_bank")
            return bank

        grouped = {}
        codes = {}

        def transpose_half(key, half, engine):
            blocks = unit_blocks(key)
            if half == 0:
                grouped[key] = grouped_pool.tile([P, CHUNK, PACK], BF16, tag="unit_bf16", align_bytes=64, name="unit_bf16")
            unit_bf16 = grouped[key]
            unit_words = unit_bf16[:].bitcast(F32)
            bank = new_bank(engine)
            planes = bank[:].rearrange("p (b u r) -> p b u r", b=2, u=2)
            for b in range(2):
                for u in range(2):
                    nc.tensor.transpose(planes[:, b, u, :], blocks[2 * half + b][:, u:WORDS:2], ident[:])
            destination = unit_words[:, 2 * P * half : 2 * P * (half + 1), :].rearrange("p (b r) u -> p b r u", b=2)
            if engine == SCALAR:
                nc.scalar.copy(out=destination, in_=planes.rearrange("p b u r -> p b r u"))
            else:
                nc.vector.tensor_copy(out=destination, in_=planes.rearrange("p b u r -> p b r u"))

        def quantise(key, first=0, last=CHUNK):
            if first == 0:
                tag = key[0]
                words = codes_pool.tile([P, CHUNK], U32, tag=tag + "_words", align_bytes=64)
                scales = codes_pool.tile([P, CHUNK], U8, tag=tag + "_scales", align_bytes=64)
                codes[key] = (words, scales)
            words, scales = codes[key]
            nc.vector.quantize_mx(
                out=words[:, first:last].bitcast(FP8X4),
                scales=scales[:, first:last],
                in_=grouped[key][:, first:last, :].rearrange("p c j -> p (c j)"),
            )

        planar = {}

        def layer1_pass(s, c, j, tokens, out):
            x_words, x_scales = codes[("x", s)]
            w_words, w_scales = codes[("w1", s // CHUNKS_PER_GROUP, c)]
            nc.tensor.matmul_mx(
                out=out,
                lhsT=w_words[:, j * P : (j + 1) * P].bitcast(FP8X4),
                lhsT_scale=w_scales[:, j * P : (j + 1) * P],
                rhs=x_words[:, tokens].bitcast(FP8X4),
                rhs_scale=x_scales[:, tokens],
                start=True,
                stop=True,
            )

        def bias1(s, c):
            first = INNER_TILES * (s // CHUNKS_PER_GROUP) + PACK * c
            return b1_col[:, first : first + PACK]

        def layer1_scalar(s, c, j, tokens):
            if j == 0:
                planar[(s, c)] = y_pool.tile([P, PACK, CHUNK], BF16, tag="y_planar", name="y_planar")
            acc1 = new_bank(SCALAR)
            width = tokens.stop - tokens.start
            layer1_pass(s, c, j, tokens, acc1[:, 0:width])
            nc.scalar.activation(
                out=planar[(s, c)][:, j, tokens],
                in_=acc1[:, 0:width],
                func=mybir.ActivationFunctionType.Identity,
                bias=bias1(s, c)[:, j : j + 1],
            )

        def layer1_vector(s, c, tokens):
            acc1 = new_bank(VECTOR)
            tiles = acc1[:].rearrange("p (j t) -> p j t", j=PACK)
            for j in range(PACK):
                layer1_pass(s, c, j, tokens, tiles[:, j, :])
            nc.vector.tensor_tensor(
                out=word_order(s, c)[:, tokens, :],
                in0=tiles.rearrange("p j t -> p t j"),
                in1=bias1(s, c).unsqueeze(1).to_broadcast([P, P, PACK]),
                op=mybir.AluOpType.add,
            )

        def word_order(s, c):
            if ("y", s, c) not in grouped:
                y_bf16 = y_pool.tile([P, CHUNK, PACK], BF16, tag="y_bf16", align_bytes=64, name="y_bf16")
                grouped[("y", s, c)] = y_bf16
            return grouped[("y", s, c)]

        def regroup_y(s, c, last_token=CHUNK, shared=False):
            regrouped = word_order(s, c)[:].rearrange("p (t i) j -> p t j i", i=4)
            source = planar[(s, c)][:].rearrange("p j (t i) -> p t j i", i=4)
            end = last_token // 4
            if shared:
                for first, last in ((0, end // 2), (end // 2, end)):
                    nc.scalar.copy(out=regrouped[:, first:last, :, :], in_=source[:, first:last, :, :])
            else:
                nc.vector.tensor_copy(out=regrouped[:, 0:end, :, :], in_=source[:, 0:end, :, :])

        def layer2_pass(s, b, c, acc2):
            g = s // CHUNKS_PER_GROUP
            y_words, y_scales = codes[("y", s, c)]
            w_words, w_scales = codes[("w2", g, c)]
            nc.tensor.matmul_mx(
                out=acc2[:],
                lhsT=y_words[:, b * P : (b + 1) * P].bitcast(FP8X4),
                lhsT_scale=y_scales[:, b * P : (b + 1) * P],
                rhs=w_words[:].bitcast(FP8X4),
                rhs_scale=w_scales[:],
                start=(c == 0),
                stop=(c == PASSES_2 - 1),
            )

        def add_bias2(s, acc2, engine, columns=slice(0, HIDDEN)):
            g = s // CHUNKS_PER_GROUP
            bias = b2_all[:, g * HIDDEN : (g + 1) * HIDDEN][:, columns]
            acc2 = acc2[:, columns]
            width = columns.stop - columns.start
            result = out_pool.tile([P, width], F32, tag="result", name="result")
            if engine == VECTOR:
                nc.vector.tensor_tensor(out=result[:], in0=acc2, in1=bias, op=mybir.AluOpType.add)
            else:
                product = product_pool.tile([P, width], F32, tag="product", name="product")
                nc.scalar.copy(out=product[:], in_=acc2)
                nc.gpsimd.tensor_tensor(out=result[:], in0=product[:], in1=bias, op=mybir.AluOpType.add)
            return result

        def store(s, b, result, columns=slice(0, HIDDEN)):
            g, n = divmod(s, CHUNKS_PER_GROUP)
            nc.sync.dma_start(out=out_view[g, :, n * BLOCKS + b, columns], in_=result[:])

        def layer2(s, b, engine=VECTOR):
            acc2 = new_bank(engine)
            for c in range(PASSES_2):
                layer2_pass(s, b, c, acc2)
            return add_bias2(s, acc2, engine)

        halves = [(key, half) for key in units for half in range(2)]
        progress = {"halves": 0, "quantised": 0}

        def transpose_next(engine=SCALAR):
            if progress["halves"] < len(halves):
                key, half = halves[progress["halves"]]
                transpose_half(key, half, engine)
                progress["halves"] += 1

        def quantise_next():
            if 2 * progress["quantised"] + 2 <= progress["halves"]:
                quantise(units[progress["quantised"]])
                progress["quantised"] += 1

        keep_warm(WARM_UP, BANK)
        for i in range(LEAD):
            transpose_next()
            if i > 0:
                quantise_next()
            transpose_next(VECTOR if i == 1 else SCALAR)
            keep_warm(1, BANK // 2)
            if i == 2:
                transpose_bias()
        quantise_next()

        rounds = CHUNKS * PASSES_2
        every_token = slice(0, CHUNK)
        for n in range(rounds - 1):
            s, c = divmod(n, PASSES_2)
            behind = n >= LAG
            scalar_tokens = every_token if behind else slice(0, CHUNK // 2)
            for pair in range(2):
                layer1_scalar(s, c, 2 * pair, scalar_tokens)
                layer1_scalar(s, c, 2 * pair + 1, scalar_tokens)
                if behind:
                    earlier, half = divmod(n - LAG, 2)
                    store(earlier, 2 * half + pair, layer2(earlier, 2 * half + pair))
                else:
                    layer1_vector(s, c, slice((2 + pair) * P, (3 + pair) * P))
            for i in range(HALVES_PER_ROUND):
                transpose_next()
            regroup_y(s, c, scalar_tokens.stop)
            quantise_next()
            if n < rounds - 2:
                quantise(("y", s, c))
            if c == 1:
                quantise_next()

        last, before = CHUNKS - 1, CHUNKS - 2
        for pair in range(2):
            layer1_scalar(last, 1, 2 * pair, every_token)
            layer1_scalar(last, 1, 2 * pair + 1, every_token)
            if pair == 0:
                store(before, 0, layer2(before, 0))
                quantise(("y", last, 0))
        regroup_y(last, 1, shared=True)
        store(before, 1, layer2(before, 1))
        store(before, 2, layer2(before, 2))
        quantise(("y", last, 1), 0, CHUNK // 2)
        store(before, 3, layer2(before, 3))
        quantise(("y", last, 1), CHUNK // 2, CHUNK)
        accs = [new_bank(SCALAR) for b in range(BLOCKS)]
        for c in range(PASSES_2):
            for b in range(BLOCKS):
                layer2_pass(last, b, c, accs[b])
        for b in range(BLOCKS):
            if b < BLOCKS - 1:
                store(last, b, add_bias2(last, accs[b], VECTOR))
            else:
                for half in range(2):
                    columns = slice(half * HIDDEN // 2, (half + 1) * HIDDEN // 2)
                    store(last, b, add_bias2(last, accs[b], VECTOR, columns), columns)
